import numpy as np
import ml_dtypes


def mxq(x, axis, fmt="e4m3"):
    dtype, down = {"e4m3": (ml_dtypes.float8_e4m3fn, 7), "e5m2": (ml_dtypes.float8_e5m2, 14)}[fmt]
    v = np.moveaxis(np.asarray(x, np.float32).astype(ml_dtypes.bfloat16).astype(np.float64), axis, -1)
    blocks = v.reshape(v.shape[:-1] + (-1, 32))
    amax = np.abs(blocks).max(-1, keepdims=True)
    byte = np.maximum(np.where(amax > 0, np.frexp(amax)[1] - 1 + 127, 0) - down, 1)
    scale = np.exp2(byte - 127.0)
    codes = (blocks / scale).astype(np.float32).astype(dtype).astype(np.float64)
    return np.moveaxis((codes * scale).reshape(v.shape), -1, axis)


WIDE = False


def mx_kscale(k):
    if not WIDE:
        return np.ones(k)
    levels = np.array([10, -10, 5, -5, 0])
    a = np.random.permutation(np.resize(levels, k // 512 * 4)).reshape(k // 512, 4)
    idx = np.arange(k)
    return np.exp2(a[idx // 512, idx % 128 // 32])


BF16 = ml_dtypes.bfloat16


def bf(x):
    return np.asarray(x, np.float32).astype(BF16)


def f64(x):
    return np.asarray(x).astype(np.float64)


E2M1 = np.array([0.0, 0.5, 1.0, 1.5, 2.0, 3.0, 4.0, 6.0, -0.0, -0.5, -1.0, -1.5, -2.0, -3.0, -4.0, -6.0])


def pack_weight(w, fmt):
    k, n = w.shape
    w = f64(bf(w)).reshape(k // 32, 32, n)
    amax = np.abs(w).max(1)
    if fmt == "e4m3":
        byte = np.frexp(amax)[1] - 1 + 127 - 7
    else:
        mant, ex = np.frexp(amax / 6.0)
        byte = np.where(mant > 0.5, ex, ex - 1) + 127
    byte = np.clip(np.where(amax > 0, byte, 1), 1, 254)
    scaled = (w * np.exp2(127.0 - byte)[:, None, :]).reshape(k, n).astype(np.float32)
    by_word = np.ascontiguousarray(scaled.reshape(k // 512, 128, 4, n).transpose(0, 1, 3, 2))
    if fmt == "e4m3":
        words = by_word.astype(ml_dtypes.float8_e4m3fn).view(np.uint8)
    else:
        c = by_word.astype(ml_dtypes.float4_e2m1fn).view(np.uint8) & 0xF
        words = c[..., 0::2] | (c[..., 1::2] << 4)
    return np.ascontiguousarray(words), np.ascontiguousarray(byte.astype(np.uint8).reshape(k // 512, 16, n))


def unpack_weight(words, scales, fmt):
    g, p, n, _ = words.shape
    if fmt == "e4m3":
        vals = np.ascontiguousarray(words).view(ml_dtypes.float8_e4m3fn).astype(np.float64)
    else:
        nib = np.empty((g, p, n, 4), np.uint8)
        nib[..., 0::2] = words & 0xF
        nib[..., 1::2] = words >> 4
        vals = E2M1[nib]
    vals = vals * np.repeat(np.exp2(scales.astype(np.float64) - 127.0), 8, axis=1)[..., None]
    return vals.transpose(0, 1, 3, 2).reshape(g * 512, n)


N, D, M, P = 128, 8, 4096, 4096


def setup_inputs():
    a = np.log2(mx_kscale(M))
    a = a.max() - a
    x = np.random.standard_normal((N, D))
    z = np.random.uniform(0.0, 1.0, (M, D))
    z[:, 0] += a * np.log(2.0)
    g = np.random.standard_normal((M, P)) * 3.2 / np.sqrt(M)
    c = np.triu(g) + 0.25 * np.tril(g, -1) + np.eye(M, P)
    words, scales = pack_weight(c * np.exp2(a)[:, None], "e4m3")
    return {"x": bf(x), "design_points": bf(z), "chol_inv_words": words, "chol_inv_scales": scales}


def reference(x, design_points, chol_inv_words, chol_inv_scales):
    x = f64(x)
    z = f64(design_points)
    mn = np.min(x, axis=0, keepdims=True)
    mx = np.max(x, axis=0, keepdims=True)
    xs = (x - mn) / (mx - mn)
    l1 = np.zeros((x.shape[0], z.shape[0]))
    for d in range(D):
        l1 = l1 + np.abs(xs[:, d][:, None] - z[:, d][None, :])
    k_star = np.exp(-l1)
    return mxq(k_star, 1, "e4m3") @ unpack_weight(chol_inv_words, chol_inv_scales, "e4m3")

@@ -1,0 +1,314 @@
+from contextlib import ExitStack
+
+import concourse.mybir as mybir
+from concourse.masks import make_identity
+
+F32 = mybir.dt.float32
+BF16 = mybir.dt.bfloat16
+I32 = mybir.dt.int32
+U8 = mybir.dt.uint8
+U32 = mybir.dt.uint32
+FP8X4 = mybir.dt.float8_e4m3fn_x4
+ALU = mybir.AluOpType
+ACT = mybir.ActivationFunctionType
+AX = mybir.AxisListType
+
+P = 128
+N = 128
+D = 8
+G = 8
+T = 4
+CW = 512
+C = 8
+CA = 6
+VG = (0, 2, 4, 5, 7)
+AG = (1, 3, 6)
+STEP = 3
+RUN = 3
+LAG = 4
+FLOPS = 2 * 128 * 4096 * 4096
+
+
+def tile_tmgp_sg_w_kernel(tc, x, design_points, chol_inv_words, chol_inv_scales, out):
+    nc = tc.nc
+    with ExitStack() as ctx:
+        const = ctx.enter_context(tc.tile_pool(name="const", bufs=1))
+        work = ctx.enter_context(tc.tile_pool(name="work", bufs=3))
+        plane = ctx.enter_context(tc.tile_pool(name="plane", bufs=24))
+        outp = ctx.enter_context(tc.tile_pool(name="outp", bufs=8))
+        psum = ctx.enter_context(tc.psum_pool(name="psum", bufs=1))
+        ctx.enter_context(tc.manual_schedule())
+
+        xn = const.tile([P, D], BF16)
+        nc.scalar.dma_start(out=xn[:], in_=x[:, :])
+        zn = const.tile([P, G, T * D], BF16)
+        nc.scalar.dma_start(
+            out=zn[:], in_=design_points.rearrange("(g p t) d -> p g (t d)", g=G, p=P, t=T)
+        )
+
+        planes = []
+        for h in range(2):
+            sp = const.tile([P, C * CW], U8, name="sp%d" % h, align_bytes=64)
+            nc.vector.memset(sp[:].bitcast(I32), 0)
+            planes.append(sp)
+        for h in range(2):
+            for q in range(4):
+                nc.sync.dma_start(
+                    out=planes[h][32 * q : 32 * q + 16, :].bitcast(I32),
+                    in_=chol_inv_scales[4 * h : 4 * h + 4, 4 * q : 4 * q + 4, :].bitcast(I32),
+                )
+        words = []
+        for g in range(G):
+            wt = const.tile([P, C * CW], I32, name="w%d" % g, align_bytes=64)
+            src = chol_inv_words[g].rearrange("p n t -> p (n t)")
+            pieces = 2 if g == G - 1 else 1
+            wid = C * CW // pieces
+            for k in range(pieces):
+                nc.sync.dma_start(
+                    out=wt[:, k * wid : (k + 1) * wid],
+                    in_=src[:, 4 * k * wid : 4 * (k + 1) * wid].bitcast(I32),
+                )
+            words.append(wt)
+
+        ident = const.tile([P, P], BF16)
+        make_identity(nc, ident[:])
+        ident_f = const.tile([P, P], F32)
+        make_identity(nc, ident_f[:])
+        warm = const.tile([P, 2], F32)
+        nc.vector.memset(warm[:], 0.0)
+        nc.scalar.activation(out=warm[:, 1:2], in_=warm[:, 0:1], func=ACT.Exp)
+
+        zf = const.tile([P, G, T * D], F32)
+        nc.gpsimd.tensor_scalar(out=zf[:], in0=zn[:], scalar1=1.0, scalar2=0.0, op0=ALU.mult, op1=ALU.add)
+        nhz = const.tile([P, G, T * D], F32)
+        nc.gpsimd.tensor_scalar(out=nhz[:], in0=zn[:], scalar1=-0.5, scalar2=0.0, op0=ALU.mult, op1=ALU.add)
+        z4 = zf[:].rearrange("p g (t d) -> p g t d", t=T)
+        nhz4 = nhz[:].rearrange("p g (t d) -> p g t d", t=T)
+
+        xrep = const.tile([P, 16, D], BF16)
+        nc.vector.tensor_copy(out=xrep[:], in_=xn[:].unsqueeze(1).to_broadcast([P, 16, D]))
+        xt_ps = psum.tile([P, N], BF16, name="xt_ps", tag="b2")
+        nc.tensor.transpose(out=xt_ps[:], in_=xrep[:].rearrange("p r d -> p (r d)"), identity=ident[:])
+        xb = []
+
+        def spread_x(half):
+            xbt = psum.tile([P, 4, N], F32, name="xb%d" % half, tag="b%d" % half)
+            for i in range(4):
+                d = 4 * half + i
+                nc.tensor.matmul(
+                    out=xbt[:, i, :],
+                    lhsT=xn[:, d : d + 1].to_broadcast([P, P]),
+                    rhs=ident[:],
+                    start=True,
+                    stop=True,
+                )
+            xb.append(xbt)
+
+        spread_x(0)
+        st = const.tile([P, 2], F32)
+        nc.vector.tensor_reduce(out=st[:, 0:1], in_=xt_ps[:], axis=AX.X, op=ALU.min)
+        nc.vector.tensor_reduce(out=st[:, 1:2], in_=xt_ps[:], axis=AX.X, op=ALU.max)
+        st_b = const.tile([P, 2], BF16)
+        nc.vector.tensor_copy(out=st_b[:], in_=st[:])
+        mm = psum.tile([P, 2, D], F32, name="mm", tag="b3")
+        for k in range(2):
+            nc.tensor.matmul(
+                out=mm[:, k, :],
+                lhsT=st_b[:, k : k + 1].to_broadcast([P, P]),
+                rhs=ident[:, 0:D],
+                start=True,
+                stop=True,
+            )
+        spread_x(1)
+        nsz = const.tile([P, G * T], F32)
+        nc.vector.tensor_reduce(
+            out=nsz[:], in_=nhz[:].rearrange("p g (t d) -> p (g t) d", t=T), axis=AX.X, op=ALU.add
+        )
+        mn = const.tile([P, D], F32)
+        nc.vector.tensor_copy(out=mn[:], in_=mm[:, 0, :])
+        inv = const.tile([P, D], F32)
+        nc.vector.tensor_tensor(out=inv[:], in0=mm[:, 1, :], in1=mn[:], op=ALU.subtract)
+        nc.vector.reciprocal(out=inv[:], in_=inv[:])
+        xsb = const.tile([P, D, N], F32)
+        for d in range(D):
+            nc.vector.tensor_scalar(
+                out=xsb[:, d, :],
+                in0=xb[d // 4][:, d % 4, :],
+                scalar1=mn[:, d : d + 1],
+                scalar2=inv[:, d : d + 1],
+                op0=ALU.subtract,
+                op1=ALU.mult,
+            )
+        sx_ps = psum.tile([P, P], F32, name="sx_ps", tag="b4")
+        for d in range(D):
+            nc.tensor.matmul(
+                out=sx_ps[:], lhsT=xsb[:, d, :], rhs=ident_f[:], is_transpose=True,
+                start=(d == 0), stop=(d == D - 1),
+            )
+        nh1 = const.tile([P, P], F32)
+        ng_ps = psum.tile([P, P], F32, name="ng_ps", tag="b5")
+        negh = const.tile([P, N], F32)
+
+        kw = const.tile([P, G, N], U32, align_bytes=64)
+        ks = const.tile([P, G, N], U8, align_bytes=64)
+
+        def quantise(grp, g):
+            nc.vector.quantize_mx(
+                out=kw[:, g, :].bitcast(FP8X4),
+                scales=ks[:, g, :],
+                in_=grp[:].rearrange("p n t -> p (n t)"),
+            )
+
+        accs = {}
+
+        def mx_pass(g, c):
+            if g == 0:
+                accs[c] = psum.tile([P, CW], F32, name="o%d" % c, tag="b%d" % c)
+            k = 4 * (g % 4)
+            nc.tensor.matmul_mx(
+                out=accs[c][:],
+                lhsT=kw[:, g, :].bitcast(FP8X4),
+                lhsT_scale=ks[:, g, :],
+                rhs=words[g][:, c * CW : (c + 1) * CW].bitcast(FP8X4),
+                rhs_scale=planes[g // 4][k:P, c * CW : (c + 1) * CW],
+                start=(g == 0),
+                stop=(g == G - 1),
+            )
+
+        def store(c):
+            res = outp.tile([P, CW], F32, name="res%d" % c, tag="res")
+            if c % 2 == 0:
+                nc.scalar.copy(out=res[:], in_=accs[c][:])
+            else:
+                nc.vector.tensor_copy(out=res[:], in_=accs[c][:])
+            nc.sync.dma_start(out=out[:, c * CW : (c + 1) * CW], in_=res[:])
+
+        def make_planes(period):
+            ga = AG[period // T]
+            t = period % T
+            made = []
+            for d in range(D):
+                pl = plane.tile([P, N], F32, name="pl%d_%d" % (period, d), tag="pl")
+                nc.scalar.activation(
+                    out=pl[:], in_=xsb[:, d, :], func=ACT.Abs, bias=nhz4[:, ga, t, d : d + 1], scale=0.5
+                )
+                made.append(pl)
+            return made
+
+        def start_tile(g):
+            acc = work.tile([P, T, N], F32, name="acc%d" % g, tag="acc")
+            for t in range(T):
+                nc.scalar.activation(
+                    out=acc[:, t, :], in_=negh[:], func=ACT.Identity,
+                    bias=nsz[:, g * T + t : g * T + t + 1], scale=1.0,
+                )
+            return acc
+
+        def vector_round(acc, gv, s):
+            for t in range(T):
+                if s == 0 and gv == VG[0]:
+                    nc.vector.tensor_scalar(
+                        out=acc[:, t, :],
+                        in0=xsb[:, 0, :],
+                        scalar1=z4[:, gv, t, 0:1],
+                        scalar2=nsz[:, gv * T + t : gv * T + t + 1],
+                        op0=ALU.max,
+                        op1=ALU.add,
+                    )
+                else:
+                    nc.vector.scalar_tensor_tensor(
+                        out=acc[:, t, :],
+                        in0=xsb[:, s, :],
+                        scalar=z4[:, gv, t, s : s + 1],
+                        in1=acc[:, t, :],
+                        op0=ALU.max,
+                        op1=ALU.add,
+                    )
+
+        def regroup(xt, g):
+            grp = work.tile([P, N, T], BF16, name="grp%d" % g, tag="grp", align_bytes=64)
+            nc.scalar.copy(out=grp[:], in_=xt[:].rearrange("p t n -> p n t"))
+            return grp
+
+        periods = len(AG) * T
+        early = [(g, c) for g in range(4) for c in range(CA)]
+
+        def mx_run():
+            for g, c in early[:RUN]:
+                mx_pass(g, c)
+            early[:RUN] = []
+
+        planes_now = make_planes(0)
+        acc_v = work.tile([P, T, N], F32, name="acc%d" % VG[0], tag="acc")
+        acc_next = None
+        acc_a = None
+        xt = None
+        regroup_at = {}
+        quantise_at = {}
+        for slot in range(len(VG) * D):
+            j = slot // D
+            s = slot % D
+            gv = VG[j]
+            if slot % STEP == 0 and slot // STEP <= periods:
+                period = slot // STEP
+                i = period // T
+                r = period % T
+                if period < periods:
+                    if r == 0:
+                        acc_a = psum.tile([P, T * P], F32, name="hl%d" % i, tag="b7")
+                    for d in range(D):
+                        nc.tensor.matmul(
+                            out=acc_a[:, r * P : (r + 1) * P], lhsT=planes_now[d][:], rhs=ident_f[:],
+                            is_transpose=True, start=(d == 0), stop=(d == D - 1),
+                        )
+                    if period == 1:
+                        nc.tensor.transpose(out=ng_ps[:], in_=nh1[:], identity=ident_f[:])
+                    if period >= LAG:
+                        mx_run()
+                if period + 1 < periods:
+                    planes_now = make_planes(period + 1)
+                if period == 0:
+                    nc.scalar.activation(out=nh1[:], in_=sx_ps[:], func=ACT.Copy, scale=-0.5)
+                if period == 1:
+                    nc.scalar.copy(out=negh[:], in_=ng_ps[:])
+                if period in regroup_at:
+                    g = regroup_at[period]
+                    quantise_at[slot + 2] = (regroup(xt, g), g)
+                if period < periods and r == T - 1:
+                    kn = work.tile([P, T * P], BF16, name="kn%d" % i, tag="kn")
+                    nc.scalar.activation(out=kn[:], in_=acc_a[:], func=ACT.Exp, scale=-2.0)
+                    xt = psum.tile([P, T, N], BF16, name="xt%d" % i, tag="b6")
+                    for t in range(T):
+                        nc.tensor.transpose(out=xt[:, t, :], in_=kn[:, t * P : (t + 1) * P], identity=ident[:])
+                    regroup_at[period + 1] = AG[i]
+            vector_round(acc_v, gv, s)
+            if slot in quantise_at:
+                quantise(quantise_at[slot][0], quantise_at[slot][1])
+            if s == 4 and j + 1 < len(VG):
+                acc_next = start_tile(VG[j + 1])
+            if s == D - 1:
+                if j == 0:
+                    nc.vector.tensor_tensor(
+                        out=acc_v[:], in0=acc_v[:], in1=negh[:].unsqueeze(1).to_broadcast([P, T, N]), op=ALU.add
+                    )
+                grp_v = work.tile([P, N, T], BF16, name="grp%d" % gv, tag="grp", align_bytes=64)
+                nc.scalar.activation(
+                    out=grp_v[:], in_=acc_v[:].rearrange("p t n -> p n t"), func=ACT.Exp, scale=-2.0
+                )
+                if j + 1 < len(VG):
+                    quantise_at[slot + 2] = (grp_v, gv)
+                else:
+                    quantise(grp_v, gv)
+                acc_v = acc_next
+
+        for c in range(CA):
+            mx_pass(4, c)
+        for c in (C - 1, C - 2):
+            for g in range(5):
+                mx_pass(g, c)
+        for g in (5, 6):
+            for c in range(C):
+                mx_pass(g, c)
+        for c in range(C):
+            mx_pass(G - 1, c)
+            store(c)

@@ -51,12 +51,14 @@ def tile_tmgp_sg_w_kernel(tc, x, design_points, chol_inv_words, chol_inv_scales,
             sp = const.tile([P, C * CW], U8, name="sp%d" % h, align_bytes=64)
             nc.vector.memset(sp[:].bitcast(I32), 0)
             planes.append(sp)
+        half = C * CW // 2
         for h in range(2):
-            for q in range(4):
-                nc.sync.dma_start(
-                    out=planes[h][32 * q : 32 * q + 16, :].bitcast(I32),
-                    in_=chol_inv_scales[4 * h : 4 * h + 4, 4 * q : 4 * q + 4, :].bitcast(I32),
-                )
+            for u in range(2):
+                for q in range(4):
+                    nc.sync.dma_start(
+                        out=planes[h][32 * q : 32 * q + 16, u * half : (u + 1) * half].bitcast(I32),
+                        in_=chol_inv_scales[4 * h : 4 * h + 4, 4 * q : 4 * q + 4, u * half : (u + 1) * half].bitcast(I32),
+                    )
         words = []
         for g in range(G):
             wt = const.tile([P, C * CW], I32, name="w%d" % g, align_bytes=64)

@@ -63,7 +63,7 @@ def tile_tmgp_sg_w_kernel(tc, x, design_points, chol_inv_words, chol_inv_scales,
         for g in range(G):
             wt = const.tile([P, C * CW], I32, name="w%d" % g, align_bytes=64)
             src = chol_inv_words[g].rearrange("p n t -> p (n t)")
-            pieces = 2 if g == G - 1 else 1
+            pieces = 4 if g == G - 1 else 1
             wid = C * CW // pieces
             for k in range(pieces):
                 nc.sync.dma_start(
@@ -308,9 +308,9 @@ def tile_tmgp_sg_w_kernel(tc, x, design_points, chol_inv_words, chol_inv_scales,
         for c in (C - 1, C - 2):
             for g in range(5):
                 mx_pass(g, c)
-        for g in (5, 6):
-            for c in range(C):
-                mx_pass(g, c)
         for c in range(C):
+            mx_pass(5, c)
+        for c in range(C):
+            mx_pass(6, c)
             mx_pass(G - 1, c)
             store(c)

@@ -52,13 +52,16 @@ def tile_tmgp_sg_w_kernel(tc, x, design_points, chol_inv_words, chol_inv_scales,
             nc.vector.memset(sp[:].bitcast(I32), 0)
             planes.append(sp)
         half = C * CW // 2
-        for h in range(2):
-            for u in range(2):
-                for q in range(4):
-                    nc.sync.dma_start(
-                        out=planes[h][32 * q : 32 * q + 16, u * half : (u + 1) * half].bitcast(I32),
-                        in_=chol_inv_scales[4 * h : 4 * h + 4, 4 * q : 4 * q + 4, u * half : (u + 1) * half].bitcast(I32),
-                    )
+        for pair in ((2, 3), (0, 1)):
+            for h in range(2):
+                for u in range(2):
+                    for q in pair:
+                        nc.sync.dma_start(
+                            out=planes[h][32 * q : 32 * q + 16, u * half : (u + 1) * half].bitcast(I32),
+                            in_=chol_inv_scales[
+                                4 * h : 4 * h + 4, 4 * q : 4 * q + 4, u * half : (u + 1) * half
+                            ].bitcast(I32),
+                        )
         words = []
         for g in range(G):
             wt = const.tile([P, C * CW], I32, name="w%d" % g, align_bytes=64)

@@ -51,17 +51,13 @@ def tile_tmgp_sg_w_kernel(tc, x, design_points, chol_inv_words, chol_inv_scales,
             sp = const.tile([P, C * CW], U8, name="sp%d" % h, align_bytes=64)
             nc.vector.memset(sp[:].bitcast(I32), 0)
             planes.append(sp)
-        half = C * CW // 2
         for pair in ((2, 3), (0, 1)):
             for h in range(2):
-                for u in range(2):
-                    for q in pair:
-                        nc.sync.dma_start(
-                            out=planes[h][32 * q : 32 * q + 16, u * half : (u + 1) * half].bitcast(I32),
-                            in_=chol_inv_scales[
-                                4 * h : 4 * h + 4, 4 * q : 4 * q + 4, u * half : (u + 1) * half
-                            ].bitcast(I32),
-                        )
+                for q in pair:
+                    nc.sync.dma_start(
+                        out=planes[h][32 * q : 32 * q + 16, :].bitcast(I32),
+                        in_=chol_inv_scales[4 * h : 4 * h + 4, 4 * q : 4 * q + 4, :].bitcast(I32),
+                    )
         words = []
         for g in range(G):
             wt = const.tile([P, C * CW], I32, name="w%d" % g, align_bytes=64)

@@ -49,15 +49,19 @@ def tile_tmgp_sg_w_kernel(tc, x, design_points, chol_inv_words, chol_inv_scales,
         planes = []
         for h in range(2):
             sp = const.tile([P, C * CW], U8, name="sp%d" % h, align_bytes=64)
-            nc.vector.memset(sp[:].bitcast(I32), 0)
             planes.append(sp)
+        nc.vector.memset(planes[1][:].bitcast(I32), 0)
         for pair in ((2, 3), (0, 1)):
-            for h in range(2):
-                for q in pair:
-                    nc.sync.dma_start(
-                        out=planes[h][32 * q : 32 * q + 16, :].bitcast(I32),
-                        in_=chol_inv_scales[4 * h : 4 * h + 4, 4 * q : 4 * q + 4, :].bitcast(I32),
-                    )
+            for q in pair:
+                nc.sync.dma_start(
+                    out=planes[0][32 * q : 32 * q + 32, :].bitcast(I32),
+                    in_=chol_inv_scales[:, 4 * q : 4 * q + 4, :].bitcast(I32),
+                )
+            for q in pair:
+                nc.sync.dma_start(
+                    out=planes[1][32 * q : 32 * q + 16, :].bitcast(I32),
+                    in_=chol_inv_scales[4:8, 4 * q : 4 * q + 4, :].bitcast(I32),
+                )
         words = []
         for g in range(G):
             wt = const.tile([P, C * CW], I32, name="w%d" % g, align_bytes=64)
@@ -79,12 +83,7 @@ def tile_tmgp_sg_w_kernel(tc, x, design_points, chol_inv_words, chol_inv_scales,
         nc.vector.memset(warm[:], 0.0)
         nc.scalar.activation(out=warm[:, 1:2], in_=warm[:, 0:1], func=ACT.Exp)
 
-        zf = const.tile([P, G, T * D], F32)
-        nc.gpsimd.tensor_scalar(out=zf[:], in0=zn[:], scalar1=1.0, scalar2=0.0, op0=ALU.mult, op1=ALU.add)
-        nhz = const.tile([P, G, T * D], F32)
-        nc.gpsimd.tensor_scalar(out=nhz[:], in0=zn[:], scalar1=-0.5, scalar2=0.0, op0=ALU.mult, op1=ALU.add)
-        z4 = zf[:].rearrange("p g (t d) -> p g t d", t=T)
-        nhz4 = nhz[:].rearrange("p g (t d) -> p g t d", t=T)
+        z4 = zn[:].rearrange("p g (t d) -> p g t d", t=T)
 
         xrep = const.tile([P, 16, D], BF16)
         nc.vector.tensor_copy(out=xrep[:], in_=xn[:].unsqueeze(1).to_broadcast([P, 16, D]))
@@ -123,8 +122,11 @@ def tile_tmgp_sg_w_kernel(tc, x, design_points, chol_inv_words, chol_inv_scales,
         spread_x(1)
         nsz = const.tile([P, G * T], F32)
         nc.vector.tensor_reduce(
-            out=nsz[:], in_=nhz[:].rearrange("p g (t d) -> p (g t) d", t=T), axis=AX.X, op=ALU.add
+            out=nsz[:], in_=zn[:].rearrange("p g (t d) -> p (g t) d", t=T), axis=AX.X, op=ALU.add
         )
+        z0f = const.tile([P, T], F32)
+        nc.vector.tensor_copy(out=z0f[:], in_=z4[:, VG[0], :, 0])
+        nc.vector.tensor_scalar(out=nsz[:], in0=nsz[:], scalar1=-0.5, scalar2=None, op0=ALU.mult)
         mn = const.tile([P, D], F32)
         nc.vector.tensor_copy(out=mn[:], in_=mm[:, 0, :])
         inv = const.tile([P, D], F32)
@@ -191,7 +193,7 @@ def tile_tmgp_sg_w_kernel(tc, x, design_points, chol_inv_words, chol_inv_scales,
             for d in range(D):
                 pl = plane.tile([P, N], F32, name="pl%d_%d" % (period, d), tag="pl")
                 nc.scalar.activation(
-                    out=pl[:], in_=xsb[:, d, :], func=ACT.Abs, bias=nhz4[:, ga, t, d : d + 1], scale=0.5
+                    out=pl[:], in_=xsb[:, d, :], func=ACT.Abs, bias=z4[:, ga, t, d : d + 1], scale=-1.0
                 )
                 made.append(pl)
             return made
@@ -211,7 +213,7 @@ def tile_tmgp_sg_w_kernel(tc, x, design_points, chol_inv_words, chol_inv_scales,
                     nc.vector.tensor_scalar(
                         out=acc[:, t, :],
                         in0=xsb[:, 0, :],
-                        scalar1=z4[:, gv, t, 0:1],
+                        scalar1=z0f[:, t : t + 1],
                         scalar2=nsz[:, gv * T + t : gv * T + t + 1],
                         op0=ALU.max,
                         op1=ALU.add,
@@ -277,7 +279,7 @@ def tile_tmgp_sg_w_kernel(tc, x, design_points, chol_inv_words, chol_inv_scales,
                     quantise_at[slot + 2] = (regroup(xt, g), g)
                 if period < periods and r == T - 1:
                     kn = work.tile([P, T * P], BF16, name="kn%d" % i, tag="kn")
-                    nc.scalar.activation(out=kn[:], in_=acc_a[:], func=ACT.Exp, scale=-2.0)
+                    nc.scalar.activation(out=kn[:], in_=acc_a[:], func=ACT.Exp, scale=-1.0)
                     xt = psum.tile([P, T, N], BF16, name="xt%d" % i, tag="b6")
                     for t in range(T):
                         nc.tensor.transpose(out=xt[:, t, :], in_=kn[:, t * P : (t + 1) * P], identity=ident[:])

@@ -20,6 +20,7 @@ G = 8
 T = 4
 CW = 512
 C = 8
+XV = 5
 CA = 6
 VG = (0, 2, 4, 5, 7)
 AG = (1, 3, 6)
@@ -79,6 +80,8 @@ def tile_tmgp_sg_w_kernel(tc, x, design_points, chol_inv_words, chol_inv_scales,
         make_identity(nc, ident[:])
         ident_f = const.tile([P, P], F32)
         make_identity(nc, ident_f[:])
+        nident = const.tile([P, D], BF16)
+        nc.gpsimd.tensor_scalar(out=nident[:], in0=ident[:, 0:D], scalar1=-1.0, scalar2=0.0, op0=ALU.mult, op1=ALU.add)
         warm = const.tile([P, 2], F32)
         nc.vector.memset(warm[:], 0.0)
         nc.scalar.activation(out=warm[:, 1:2], in_=warm[:, 0:1], func=ACT.Exp)
@@ -105,20 +108,14 @@ def tile_tmgp_sg_w_kernel(tc, x, design_points, chol_inv_words, chol_inv_scales,
             xb.append(xbt)
 
         spread_x(0)
-        st = const.tile([P, 2], F32)
-        nc.vector.tensor_reduce(out=st[:, 0:1], in_=xt_ps[:], axis=AX.X, op=ALU.min)
-        nc.vector.tensor_reduce(out=st[:, 1:2], in_=xt_ps[:], axis=AX.X, op=ALU.max)
-        st_b = const.tile([P, 2], BF16)
-        nc.vector.tensor_copy(out=st_b[:], in_=st[:])
+        lo = const.tile([P, 1], BF16)
+        hi = const.tile([P, 1], BF16)
+        nc.vector.tensor_reduce(out=lo[:], in_=xt_ps[:], axis=AX.X, op=ALU.min)
+        nc.vector.tensor_reduce(out=hi[:], in_=xt_ps[:], axis=AX.X, op=ALU.max)
         mm = psum.tile([P, 2, D], F32, name="mm", tag="b3")
-        for k in range(2):
-            nc.tensor.matmul(
-                out=mm[:, k, :],
-                lhsT=st_b[:, k : k + 1].to_broadcast([P, P]),
-                rhs=ident[:, 0:D],
-                start=True,
-                stop=True,
-            )
+        nc.tensor.matmul(out=mm[:, 0, :], lhsT=lo[:].to_broadcast([P, P]), rhs=ident[:, 0:D], start=True, stop=True)
+        nc.tensor.matmul(out=mm[:, 1, :], lhsT=lo[:].to_broadcast([P, P]), rhs=nident[:], start=True, stop=False)
+        nc.tensor.matmul(out=mm[:, 1, :], lhsT=hi[:].to_broadcast([P, P]), rhs=ident[:, 0:D], start=False, stop=True)
         spread_x(1)
         nsz = const.tile([P, G * T], F32)
         nc.vector.tensor_reduce(
@@ -128,20 +125,29 @@ def tile_tmgp_sg_w_kernel(tc, x, design_points, chol_inv_words, chol_inv_scales,
         nc.vector.tensor_copy(out=z0f[:], in_=z4[:, VG[0], :, 0])
         nc.vector.tensor_scalar(out=nsz[:], in0=nsz[:], scalar1=-0.5, scalar2=None, op0=ALU.mult)
         mn = const.tile([P, D], F32)
-        nc.vector.tensor_copy(out=mn[:], in_=mm[:, 0, :])
+        nc.scalar.copy(out=mn[:], in_=mm[:, 0, :])
         inv = const.tile([P, D], F32)
-        nc.vector.tensor_tensor(out=inv[:], in0=mm[:, 1, :], in1=mn[:], op=ALU.subtract)
-        nc.vector.reciprocal(out=inv[:], in_=inv[:])
+        nc.vector.reciprocal(out=inv[:], in_=mm[:, 1, :])
+        nmi = const.tile([P, D], F32)
+        nc.vector.scalar_tensor_tensor(
+            out=nmi[:], in0=mn[:], scalar=-1.0, in1=inv[:], op0=ALU.mult, op1=ALU.mult
+        )
         xsb = const.tile([P, D, N], F32)
         for d in range(D):
-            nc.vector.tensor_scalar(
-                out=xsb[:, d, :],
-                in0=xb[d // 4][:, d % 4, :],
-                scalar1=mn[:, d : d + 1],
-                scalar2=inv[:, d : d + 1],
-                op0=ALU.subtract,
-                op1=ALU.mult,
-            )
+            if d < XV:
+                nc.vector.tensor_scalar(
+                    out=xsb[:, d, :],
+                    in0=xb[d // 4][:, d % 4, :],
+                    scalar1=mn[:, d : d + 1],
+                    scalar2=inv[:, d : d + 1],
+                    op0=ALU.subtract,
+                    op1=ALU.mult,
+                )
+            else:
+                nc.scalar.activation(
+                    out=xsb[:, d, :], in_=xb[d // 4][:, d % 4, :], func=ACT.Identity,
+                    bias=nmi[:, d : d + 1], scale=inv[:, d : d + 1],
+                )
         sx_ps = psum.tile([P, P], F32, name="sx_ps", tag="b4")
         for d in range(D):
             nc.tensor.matmul(
@@ -234,12 +240,12 @@ def tile_tmgp_sg_w_kernel(tc, x, design_points, chol_inv_words, chol_inv_scales,
             return grp
 
         periods = len(AG) * T
-        early = [(g, c) for g in range(4) for c in range(CA)]
+        early = [(g, c) for g in range(5) for c in range(CA)]
 
-        def mx_run():
-            for g, c in early[:RUN]:
+        def mx_run(count):
+            for g, c in early[:count]:
                 mx_pass(g, c)
-            early[:RUN] = []
+            early[:count] = []
 
         planes_now = make_planes(0)
         acc_v = work.tile([P, T, N], F32, name="acc%d" % VG[0], tag="acc")
@@ -267,7 +273,7 @@ def tile_tmgp_sg_w_kernel(tc, x, design_points, chol_inv_words, chol_inv_scales,
                     if period == 1:
                         nc.tensor.transpose(out=ng_ps[:], in_=nh1[:], identity=ident_f[:])
                     if period >= LAG:
-                        mx_run()
+                        mx_run(3 if period < 8 else 5)
                 if period + 1 < periods:
                     planes_now = make_planes(period + 1)
                 if period == 0:
@@ -304,8 +310,7 @@ def tile_tmgp_sg_w_kernel(tc, x, design_points, chol_inv_words, chol_inv_scales,
                     quantise(grp_v, gv)
                 acc_v = acc_next
 
-        for c in range(CA):
-            mx_pass(4, c)
+        mx_run(len(early))
         for c in (C - 1, C - 2):
             for g in range(5):
                 mx_pass(g, c)

from contextlib import ExitStack

import concourse.mybir as mybir
from concourse.masks import make_identity

F32 = mybir.dt.float32
BF16 = mybir.dt.bfloat16
I32 = mybir.dt.int32
U8 = mybir.dt.uint8
U32 = mybir.dt.uint32
FP8X4 = mybir.dt.float8_e4m3fn_x4
ALU = mybir.AluOpType
ACT = mybir.ActivationFunctionType
AX = mybir.AxisListType

P = 128
N = 128
D = 8
G = 8
T = 4
CW = 512
C = 8
XV = 5
CA = 6
VG = (0, 2, 4, 5, 7)
AG = (1, 3, 6)
STEP = 3
RUN = 3
LAG = 4
FLOPS = 2 * 128 * 4096 * 4096


def tile_tmgp_sg_w_kernel(tc, x, design_points, chol_inv_words, chol_inv_scales, out):
    nc = tc.nc
    with ExitStack() as ctx:
        const = ctx.enter_context(tc.tile_pool(name="const", bufs=1))
        work = ctx.enter_context(tc.tile_pool(name="work", bufs=3))
        plane = ctx.enter_context(tc.tile_pool(name="plane", bufs=24))
        outp = ctx.enter_context(tc.tile_pool(name="outp", bufs=8))
        psum = ctx.enter_context(tc.psum_pool(name="psum", bufs=1))
        ctx.enter_context(tc.manual_schedule())

        xn = const.tile([P, D], BF16)
        nc.scalar.dma_start(out=xn[:], in_=x[:, :])
        zn = const.tile([P, G, T * D], BF16)
        nc.scalar.dma_start(
            out=zn[:], in_=design_points.rearrange("(g p t) d -> p g (t d)", g=G, p=P, t=T)
        )

        planes = []
        for h in range(2):
            sp = const.tile([P, C * CW], U8, name="sp%d" % h, align_bytes=64)
            planes.append(sp)
        nc.vector.memset(planes[1][:].bitcast(I32), 0)
        for pair in ((2, 3), (0, 1)):
            for q in pair:
                nc.sync.dma_start(
                    out=planes[0][32 * q : 32 * q + 32, :].bitcast(I32),
                    in_=chol_inv_scales[:, 4 * q : 4 * q + 4, :].bitcast(I32),
                )
            for q in pair:
                nc.sync.dma_start(
                    out=planes[1][32 * q : 32 * q + 16, :].bitcast(I32),
                    in_=chol_inv_scales[4:8, 4 * q : 4 * q + 4, :].bitcast(I32),
                )
        words = []
        for g in range(G):
            wt = const.tile([P, C * CW], I32, name="w%d" % g, align_bytes=64)
            src = chol_inv_words[g].rearrange("p n t -> p (n t)")
            pieces = 4 if g == G - 1 else 1
            wid = C * CW // pieces
            for k in range(pieces):
                nc.sync.dma_start(
                    out=wt[:, k * wid : (k + 1) * wid],
                    in_=src[:, 4 * k * wid : 4 * (k + 1) * wid].bitcast(I32),
                )
            words.append(wt)

        ident = const.tile([P, P], BF16)
        make_identity(nc, ident[:])
        ident_f = const.tile([P, P], F32)
        make_identity(nc, ident_f[:])
        nident = const.tile([P, D], BF16)
        nc.gpsimd.tensor_scalar(out=nident[:], in0=ident[:, 0:D], scalar1=-1.0, scalar2=0.0, op0=ALU.mult, op1=ALU.add)
        warm = const.tile([P, 2], F32)
        nc.vector.memset(warm[:], 0.0)
        nc.scalar.activation(out=warm[:, 1:2], in_=warm[:, 0:1], func=ACT.Exp)

        z4 = zn[:].rearrange("p g (t d) -> p g t d", t=T)

        xrep = const.tile([P, 16, D], BF16)
        nc.vector.tensor_copy(out=xrep[:], in_=xn[:].unsqueeze(1).to_broadcast([P, 16, D]))
        xt_ps = psum.tile([P, N], BF16, name="xt_ps", tag="b2")
        nc.tensor.transpose(out=xt_ps[:], in_=xrep[:].rearrange("p r d -> p (r d)"), identity=ident[:])
        xb = []

        def spread_x(half):
            xbt = psum.tile([P, 4, N], F32, name="xb%d" % half, tag="b%d" % half)
            for i in range(4):
                d = 4 * half + i
                nc.tensor.matmul(
                    out=xbt[:, i, :],
                    lhsT=xn[:, d : d + 1].to_broadcast([P, P]),
                    rhs=ident[:],
                    start=True,
                    stop=True,
                )
            xb.append(xbt)

        spread_x(0)
        lo = const.tile([P, 1], BF16)
        hi = const.tile([P, 1], BF16)
        nc.vector.tensor_reduce(out=lo[:], in_=xt_ps[:], axis=AX.X, op=ALU.min)
        nc.vector.tensor_reduce(out=hi[:], in_=xt_ps[:], axis=AX.X, op=ALU.max)
        mm = psum.tile([P, 2, D], F32, name="mm", tag="b3")
        nc.tensor.matmul(out=mm[:, 0, :], lhsT=lo[:].to_broadcast([P, P]), rhs=ident[:, 0:D], start=True, stop=True)
        nc.tensor.matmul(out=mm[:, 1, :], lhsT=lo[:].to_broadcast([P, P]), rhs=nident[:], start=True, stop=False)
        nc.tensor.matmul(out=mm[:, 1, :], lhsT=hi[:].to_broadcast([P, P]), rhs=ident[:, 0:D], start=False, stop=True)
        spread_x(1)
        nsz = const.tile([P, G * T], F32)
        nc.vector.tensor_reduce(
            out=nsz[:], in_=zn[:].rearrange("p g (t d) -> p (g t) d", t=T), axis=AX.X, op=ALU.add
        )
        z0f = const.tile([P, T], F32)
        nc.vector.tensor_copy(out=z0f[:], in_=z4[:, VG[0], :, 0])
        nc.vector.tensor_scalar(out=nsz[:], in0=nsz[:], scalar1=-0.5, scalar2=None, op0=ALU.mult)
        mn = const.tile([P, D], F32)
        nc.scalar.copy(out=mn[:], in_=mm[:, 0, :])
        inv = const.tile([P, D], F32)
        nc.vector.reciprocal(out=inv[:], in_=mm[:, 1, :])
        nmi = const.tile([P, D], F32)
        nc.vector.scalar_tensor_tensor(
            out=nmi[:], in0=mn[:], scalar=-1.0, in1=inv[:], op0=ALU.mult, op1=ALU.mult
        )
        xsb = const.tile([P, D, N], F32)
        for d in range(D):
            if d < XV:
                nc.vector.tensor_scalar(
                    out=xsb[:, d, :],
                    in0=xb[d // 4][:, d % 4, :],
                    scalar1=mn[:, d : d + 1],
                    scalar2=inv[:, d : d + 1],
                    op0=ALU.subtract,
                    op1=ALU.mult,
                )
            else:
                nc.scalar.activation(
                    out=xsb[:, d, :], in_=xb[d // 4][:, d % 4, :], func=ACT.Identity,
                    bias=nmi[:, d : d + 1], scale=inv[:, d : d + 1],
                )
        sx_ps = psum.tile([P, P], F32, name="sx_ps", tag="b4")
        for d in range(D):
            nc.tensor.matmul(
                out=sx_ps[:], lhsT=xsb[:, d, :], rhs=ident_f[:], is_transpose=True,
                start=(d == 0), stop=(d == D - 1),
            )
        nh1 = const.tile([P, P], F32)
        ng_ps = psum.tile([P, P], F32, name="ng_ps", tag="b5")
        negh = const.tile([P, N], F32)

        kw = const.tile([P, G, N], U32, align_bytes=64)
        ks = const.tile([P, G, N], U8, align_bytes=64)

        def quantise(grp, g):
            nc.vector.quantize_mx(
                out=kw[:, g, :].bitcast(FP8X4),
                scales=ks[:, g, :],
                in_=grp[:].rearrange("p n t -> p (n t)"),
            )

        accs = {}

        def mx_pass(g, c):
            if g == 0:
                accs[c] = psum.tile([P, CW], F32, name="o%d" % c, tag="b%d" % c)
            k = 4 * (g % 4)
            nc.tensor.matmul_mx(
                out=accs[c][:],
                lhsT=kw[:, g, :].bitcast(FP8X4),
                lhsT_scale=ks[:, g, :],
                rhs=words[g][:, c * CW : (c + 1) * CW].bitcast(FP8X4),
                rhs_scale=planes[g // 4][k:P, c * CW : (c + 1) * CW],
                start=(g == 0),
                stop=(g == G - 1),
            )

        def store(c):
            res = outp.tile([P, CW], F32, name="res%d" % c, tag="res")
            if c % 2 == 0:
                nc.scalar.copy(out=res[:], in_=accs[c][:])
            else:
                nc.vector.tensor_copy(out=res[:], in_=accs[c][:])
            nc.sync.dma_start(out=out[:, c * CW : (c + 1) * CW], in_=res[:])

        def make_planes(period):
            ga = AG[period // T]
            t = period % T
            made = []
            for d in range(D):
                pl = plane.tile([P, N], F32, name="pl%d_%d" % (period, d), tag="pl")
                nc.scalar.activation(
                    out=pl[:], in_=xsb[:, d, :], func=ACT.Abs, bias=z4[:, ga, t, d : d + 1], scale=-1.0
                )
                made.append(pl)
            return made

        def start_tile(g):
            acc = work.tile([P, T, N], F32, name="acc%d" % g, tag="acc")
            for t in range(T):
                nc.scalar.activation(
                    out=acc[:, t, :], in_=negh[:], func=ACT.Identity,
                    bias=nsz[:, g * T + t : g * T + t + 1], scale=1.0,
                )
            return acc

        def vector_round(acc, gv, s):
            for t in range(T):
                if s == 0 and gv == VG[0]:
                    nc.vector.tensor_scalar(
                        out=acc[:, t, :],
                        in0=xsb[:, 0, :],
                        scalar1=z0f[:, t : t + 1],
                        scalar2=nsz[:, gv * T + t : gv * T + t + 1],
                        op0=ALU.max,
                        op1=ALU.add,
                    )
                else:
                    nc.vector.scalar_tensor_tensor(
                        out=acc[:, t, :],
                        in0=xsb[:, s, :],
                        scalar=z4[:, gv, t, s : s + 1],
                        in1=acc[:, t, :],
                        op0=ALU.max,
                        op1=ALU.add,
                    )

        def regroup(xt, g):
            grp = work.tile([P, N, T], BF16, name="grp%d" % g, tag="grp", align_bytes=64)
            nc.scalar.copy(out=grp[:], in_=xt[:].rearrange("p t n -> p n t"))
            return grp

        periods = len(AG) * T
        early = [(g, c) for g in range(5) for c in range(CA)]

        def mx_run(count):
            for g, c in early[:count]:
                mx_pass(g, c)
            early[:count] = []

        planes_now = make_planes(0)
        acc_v = work.tile([P, T, N], F32, name="acc%d" % VG[0], tag="acc")
        acc_next = None
        acc_a = None
        xt = None
        regroup_at = {}
        quantise_at = {}
        for slot in range(len(VG) * D):
            j = slot // D
            s = slot % D
            gv = VG[j]
            if slot % STEP == 0 and slot // STEP <= periods:
                period = slot // STEP
                i = period // T
                r = period % T
                if period < periods:
                    if r == 0:
                        acc_a = psum.tile([P, T * P], F32, name="hl%d" % i, tag="b7")
                    for d in range(D):
                        nc.tensor.matmul(
                            out=acc_a[:, r * P : (r + 1) * P], lhsT=planes_now[d][:], rhs=ident_f[:],
                            is_transpose=True, start=(d == 0), stop=(d == D - 1),
                        )
                    if period == 1:
                        nc.tensor.transpose(out=ng_ps[:], in_=nh1[:], identity=ident_f[:])
                    if period >= LAG:
                        mx_run(3 if period < 8 else 5)
                if period + 1 < periods:
                    planes_now = make_planes(period + 1)
                if period == 0:
                    nc.scalar.activation(out=nh1[:], in_=sx_ps[:], func=ACT.Copy, scale=-0.5)
                if period == 1:
                    nc.scalar.copy(out=negh[:], in_=ng_ps[:])
                if period in regroup_at:
                    g = regroup_at[period]
                    quantise_at[slot + 2] = (regroup(xt, g), g)
                if period < periods and r == T - 1:
                    kn = work.tile([P, T * P], BF16, name="kn%d" % i, tag="kn")
                    nc.scalar.activation(out=kn[:], in_=acc_a[:], func=ACT.Exp, scale=-1.0)
                    xt = psum.tile([P, T, N], BF16, name="xt%d" % i, tag="b6")
                    for t in range(T):
                        nc.tensor.transpose(out=xt[:, t, :], in_=kn[:, t * P : (t + 1) * P], identity=ident[:])
                    regroup_at[period + 1] = AG[i]
            vector_round(acc_v, gv, s)
            if slot in quantise_at:
                quantise(quantise_at[slot][0], quantise_at[slot][1])
            if s == 4 and j + 1 < len(VG):
                acc_next = start_tile(VG[j + 1])
            if s == D - 1:
                if j == 0:
                    nc.vector.tensor_tensor(
                        out=acc_v[:], in0=acc_v[:], in1=negh[:].unsqueeze(1).to_broadcast([P, T, N]), op=ALU.add
                    )
                grp_v = work.tile([P, N, T], BF16, name="grp%d" % gv, tag="grp", align_bytes=64)
                nc.scalar.activation(
                    out=grp_v[:], in_=acc_v[:].rearrange("p t n -> p n t"), func=ACT.Exp, scale=-2.0
                )
                if j + 1 < len(VG):
                    quantise_at[slot + 2] = (grp_v, gv)
                else:
                    quantise(grp_v, gv)
                acc_v = acc_next

        mx_run(len(early))
        for c in (C - 1, C - 2):
            for g in range(5):
                mx_pass(g, c)
        for c in range(C):
            mx_pass(5, c)
        for c in range(C):
            mx_pass(6, c)
            mx_pass(G - 1, c)
            store(c)
